import numpy as np
import ml_dtypes

BF16 = ml_dtypes.bfloat16


def bf(x):
    return np.asarray(x, np.float32).astype(BF16)


def f32(x):
    return np.asarray(x, np.float32)


def f64(x):
    return np.asarray(x).astype(np.float64)


def striped(idx):
    return np.tile(idx.reshape(-1, 16).T, (8, 1))


C, S, N, GRP = 256, 512, 128, 128
EPS = 1e-8


def sgn(v):
    return np.where(v >= 0.0, 1.0, -1.0)


def setup_inputs():
    return {"base": f32(np.random.standard_normal((C, S))), "weight": f32(np.random.standard_normal((C, N))), "scales": f32(2.0 * np.random.random((C // GRP, N)) - 0.5), "offs": striped(np.random.permutation(S)[:N])}


def reference(base, weight, scales, offs):
    idx = offs[:16].T.reshape(-1)
    out = f64(base).copy()
    out[:, idx] = sgn(f64(weight)) * np.repeat(np.maximum(f64(scales), EPS), GRP, axis=0)
    return out

@@ -1,0 +1,36 @@
+import concourse.mybir as mybir
+
+F32 = mybir.dt.float32
+U16 = mybir.dt.uint16
+ALU = mybir.AluOpType
+
+P = 128
+EPS = 1e-8
+
+
+def tile_literatiquantembedding_kernel(tc, base, weight, scales, offs, out):
+    nc = tc.nc
+    features, words = base.shape
+    entries = weight.shape[1]
+    blocks = features // P
+
+    with tc.tile_pool(name="held", bufs=1) as held:
+        offsets = held.tile([P, entries // 16], U16, name="offsets")
+        nc.sync.dma_start(offsets[:], offs)
+
+        for b in range(blocks):
+            rows = slice(b * P, (b + 1) * P)
+
+            table = held.tile([P, words], F32, name=f"table{b}")
+            nc.sync.dma_start(table[:], base[rows, :])
+            signs = held.tile([P, entries], F32, name=f"signs{b}")
+            nc.scalar.dma_start(signs[:], weight[rows, :])
+            clamped = held.tile([P, entries], F32, name=f"clamped{b}")
+            nc.scalar.dma_start(clamped[:], scales[b, :].partition_broadcast(P))
+
+            nc.vector.tensor_scalar(signs[:], signs[:], 0.0, 2.0, ALU.is_ge, ALU.mult)
+            nc.vector.tensor_scalar_add(signs[:], signs[:], -1.0)
+            nc.vector.tensor_scalar_max(clamped[:], clamped[:], EPS)
+
+            nc.vector.tensor_tensor(table[:].indirect(offsets[:]), signs[:], clamped[:], ALU.mult)
+            nc.sync.dma_start(out[rows, :], table[:])

@@ -16,21 +16,24 @@ def tile_literatiquantembedding_kernel(tc, base, weight, scales, offs, out):
 
     with tc.tile_pool(name="held", bufs=1) as held:
         offsets = held.tile([P, entries // 16], U16, name="offsets")
+        signs = held.tile([P, blocks * entries], F32, name="signs")
+        clamped = held.tile([P, blocks * entries], F32, name="clamped")
+        tables = [held.tile([P, words], F32, name=f"table{b}") for b in range(blocks)]
+        queues = [nc.sync, nc.scalar]
+
         nc.sync.dma_start(offsets[:], offs)
+        nc.sync.dma_start(
+            signs[:].rearrange("p (b n) -> p b n", b=blocks), weight.rearrange("(b p) n -> p b n", p=P)
+        )
+        nc.scalar.dma_start(clamped[:], scales.rearrange("b n -> (b n)").partition_broadcast(P))
+        for b in range(blocks):
+            queues[b % 2].dma_start(tables[b][:], base[b * P : (b + 1) * P, :])
+
+        nc.vector.tensor_scalar(signs[:], signs[:], 0.0, 2.0, ALU.is_ge, ALU.mult)
+        nc.vector.tensor_scalar_add(signs[:], signs[:], -1.0)
+        nc.vector.tensor_scalar_max(clamped[:], clamped[:], EPS)
 
         for b in range(blocks):
-            rows = slice(b * P, (b + 1) * P)
-
-            table = held.tile([P, words], F32, name=f"table{b}")
-            nc.sync.dma_start(table[:], base[rows, :])
-            signs = held.tile([P, entries], F32, name=f"signs{b}")
-            nc.scalar.dma_start(signs[:], weight[rows, :])
-            clamped = held.tile([P, entries], F32, name=f"clamped{b}")
-            nc.scalar.dma_start(clamped[:], scales[b, :].partition_broadcast(P))
-
-            nc.vector.tensor_scalar(signs[:], signs[:], 0.0, 2.0, ALU.is_ge, ALU.mult)
-            nc.vector.tensor_scalar_add(signs[:], signs[:], -1.0)
-            nc.vector.tensor_scalar_max(clamped[:], clamped[:], EPS)
-
-            nc.vector.tensor_tensor(table[:].indirect(offsets[:]), signs[:], clamped[:], ALU.mult)
-            nc.sync.dma_start(out[rows, :], table[:])
+            part = slice(b * entries, (b + 1) * entries)
+            nc.vector.tensor_tensor(tables[b][:].indirect(offsets[:]), signs[:, part], clamped[:, part], ALU.mult)
+            queues[b % 2].dma_start(out[b * P : (b + 1) * P, :], tables[b][:])

@@ -19,15 +19,14 @@ def tile_literatiquantembedding_kernel(tc, base, weight, scales, offs, out):
         signs = held.tile([P, blocks * entries], F32, name="signs")
         clamped = held.tile([P, blocks * entries], F32, name="clamped")
         tables = [held.tile([P, words], F32, name=f"table{b}") for b in range(blocks)]
-        queues = [nc.sync, nc.scalar]
 
         nc.sync.dma_start(offsets[:], offs)
         nc.sync.dma_start(
             signs[:].rearrange("p (b n) -> p b n", b=blocks), weight.rearrange("(b p) n -> p b n", p=P)
         )
-        nc.scalar.dma_start(clamped[:], scales.rearrange("b n -> (b n)").partition_broadcast(P))
+        nc.sync.dma_start(clamped[:], scales.rearrange("b n -> (b n)").partition_broadcast(P))
         for b in range(blocks):
-            queues[b % 2].dma_start(tables[b][:], base[b * P : (b + 1) * P, :])
+            nc.sync.dma_start(tables[b][:], base[b * P : (b + 1) * P, :])
 
         nc.vector.tensor_scalar(signs[:], signs[:], 0.0, 2.0, ALU.is_ge, ALU.mult)
         nc.vector.tensor_scalar_add(signs[:], signs[:], -1.0)
@@ -36,4 +35,4 @@ def tile_literatiquantembedding_kernel(tc, base, weight, scales, offs, out):
         for b in range(blocks):
             part = slice(b * entries, (b + 1) * entries)
             nc.vector.tensor_tensor(tables[b][:].indirect(offsets[:]), signs[:, part], clamped[:, part], ALU.mult)
-            queues[b % 2].dma_start(out[b * P : (b + 1) * P, :], tables[b][:])
+            nc.sync.dma_start(out[b * P : (b + 1) * P, :], tables[b][:])

@@ -13,20 +13,24 @@ def tile_literatiquantembedding_kernel(tc, base, weight, scales, offs, out):
     features, words = base.shape
     entries = weight.shape[1]
     blocks = features // P
+    groups = scales.shape[0]
+    sharers = P // groups
+
+    base_blocks = base.rearrange("(p b) s -> b p s", b=blocks)
+    out_blocks = out.rearrange("(p b) s -> b p s", b=blocks)
 
     with tc.tile_pool(name="held", bufs=1) as held:
         offsets = held.tile([P, entries // 16], U16, name="offsets")
         signs = held.tile([P, blocks * entries], F32, name="signs")
-        clamped = held.tile([P, blocks * entries], F32, name="clamped")
+        clamped = held.tile([P, entries], F32, name="clamped")
         tables = [held.tile([P, words], F32, name=f"table{b}") for b in range(blocks)]
 
         nc.sync.dma_start(offsets[:], offs)
-        nc.sync.dma_start(
-            signs[:].rearrange("p (b n) -> p b n", b=blocks), weight.rearrange("(b p) n -> p b n", p=P)
-        )
-        nc.sync.dma_start(clamped[:], scales.rearrange("b n -> (b n)").partition_broadcast(P))
+        nc.sync.dma_start(signs[:], weight.rearrange("(p b) n -> p (b n)", b=blocks))
+        for g in range(groups):
+            nc.sync.dma_start(clamped[g * sharers : (g + 1) * sharers, :], scales[g].partition_broadcast(sharers))
         for b in range(blocks):
-            nc.sync.dma_start(tables[b][:], base[b * P : (b + 1) * P, :])
+            nc.sync.dma_start(tables[b][:], base_blocks[b])
 
         nc.vector.tensor_scalar(signs[:], signs[:], 0.0, 2.0, ALU.is_ge, ALU.mult)
         nc.vector.tensor_scalar_add(signs[:], signs[:], -1.0)
@@ -34,5 +38,5 @@ def tile_literatiquantembedding_kernel(tc, base, weight, scales, offs, out):
 
         for b in range(blocks):
             part = slice(b * entries, (b + 1) * entries)
-            nc.vector.tensor_tensor(tables[b][:].indirect(offsets[:]), signs[:, part], clamped[:, part], ALU.mult)
-            nc.sync.dma_start(out[b * P : (b + 1) * P, :], tables[b][:])
+            nc.vector.tensor_tensor(tables[b][:].indirect(offsets[:]), signs[:, part], clamped[:], ALU.mult)
+            nc.sync.dma_start(out_blocks[b], tables[b][:])

@@ -19,22 +19,36 @@ def tile_literatiquantembedding_kernel(tc, base, weight, scales, offs, out):
     base_blocks = base.rearrange("(p b) s -> b p s", b=blocks)
     out_blocks = out.rearrange("(p b) s -> b p s", b=blocks)
 
-    with tc.tile_pool(name="held", bufs=1) as held:
+    with tc.tile_pool(name="held", bufs=1) as held, tc.psum_pool(name="psum", bufs=1) as psum:
         offsets = held.tile([P, entries // 16], U16, name="offsets")
         signs = held.tile([P, blocks * entries], F32, name="signs")
+        scale_rows = held.tile([1, groups * entries], F32, name="scale_rows")
+        chooser = held.tile([1, groups * P], F32, name="chooser")
+        spread = psum.tile([P, entries], F32, name="spread")
         clamped = held.tile([P, entries], F32, name="clamped")
         tables = [held.tile([P, words], F32, name=f"table{b}") for b in range(blocks)]
 
+        nc.sync.dma_start(scale_rows[:], scales.rearrange("(o g) n -> o (g n)", o=1))
         nc.sync.dma_start(offsets[:], offs)
         nc.sync.dma_start(signs[:], weight.rearrange("(p b) n -> p (b n)", b=blocks))
-        for g in range(groups):
-            nc.sync.dma_start(clamped[g * sharers : (g + 1) * sharers, :], scales[g].partition_broadcast(sharers))
         for b in range(blocks):
             nc.sync.dma_start(tables[b][:], base_blocks[b])
 
+        nc.vector.memset(chooser[:], 0.0)
+        for g in range(groups):
+            nc.vector.memset(chooser[:, g * P + g * sharers : g * P + (g + 1) * sharers], 1.0)
+        for g in range(groups):
+            nc.tensor.matmul(
+                spread[:],
+                chooser[:, g * P : (g + 1) * P],
+                scale_rows[:, g * entries : (g + 1) * entries],
+                start=(g == 0),
+                stop=(g == groups - 1),
+            )
+
         nc.vector.tensor_scalar(signs[:], signs[:], 0.0, 2.0, ALU.is_ge, ALU.mult)
         nc.vector.tensor_scalar_add(signs[:], signs[:], -1.0)
-        nc.vector.tensor_scalar_max(clamped[:], clamped[:], EPS)
+        nc.vector.tensor_scalar_max(clamped[:], spread[:], EPS)
 
         for b in range(blocks):
             part = slice(b * entries, (b + 1) * entries)

@@ -22,29 +22,29 @@ def tile_literatiquantembedding_kernel(tc, base, weight, scales, offs, out):
     with tc.tile_pool(name="held", bufs=1) as held, tc.psum_pool(name="psum", bufs=1) as psum:
         offsets = held.tile([P, entries // 16], U16, name="offsets")
         signs = held.tile([P, blocks * entries], F32, name="signs")
-        scale_rows = held.tile([1, groups * entries], F32, name="scale_rows")
-        chooser = held.tile([1, groups * P], F32, name="chooser")
+        scale_rows = held.tile([groups, entries], F32, name="scale_rows")
+        chooser = held.tile([groups, P], F32, name="chooser")
         spread = psum.tile([P, entries], F32, name="spread")
         clamped = held.tile([P, entries], F32, name="clamped")
         tables = [held.tile([P, words], F32, name=f"table{b}") for b in range(blocks)]
 
-        nc.sync.dma_start(scale_rows[:], scales.rearrange("(o g) n -> o (g n)", o=1))
+        nc.sync.dma_start(scale_rows[:], scales)
         nc.sync.dma_start(offsets[:], offs)
         nc.sync.dma_start(signs[:], weight.rearrange("(p b) n -> p (b n)", b=blocks))
         for b in range(blocks):
             nc.sync.dma_start(tables[b][:], base_blocks[b])
 
-        nc.vector.memset(chooser[:], 0.0)
-        for g in range(groups):
-            nc.vector.memset(chooser[:, g * P + g * sharers : g * P + (g + 1) * sharers], 1.0)
-        for g in range(groups):
-            nc.tensor.matmul(
-                spread[:],
-                chooser[:, g * P : (g + 1) * P],
-                scale_rows[:, g * entries : (g + 1) * entries],
-                start=(g == 0),
-                stop=(g == groups - 1),
-            )
+        nc.gpsimd.memset(chooser[:], 1.0)
+        nc.gpsimd.affine_select(
+            out=chooser[:],
+            in_=chooser[:],
+            pattern=[[-1, groups], [0, sharers]],
+            compare_op=ALU.is_equal,
+            fill=0.0,
+            base=0,
+            channel_multiplier=1,
+        )
+        nc.tensor.matmul(spread[:], chooser[:], scale_rows[:], start=True, stop=True)
 
         nc.vector.tensor_scalar(signs[:], signs[:], 0.0, 2.0, ALU.is_ge, ALU.mult)
         nc.vector.tensor_scalar_add(signs[:], signs[:], -1.0)

@@ -29,8 +29,8 @@ def tile_literatiquantembedding_kernel(tc, base, weight, scales, offs, out):
         tables = [held.tile([P, words], F32, name=f"table{b}") for b in range(blocks)]
 
         nc.sync.dma_start(scale_rows[:], scales)
-        nc.sync.dma_start(offsets[:], offs)
         nc.sync.dma_start(signs[:], weight.rearrange("(p b) n -> p (b n)", b=blocks))
+        nc.sync.dma_start(offsets[:], offs)
         for b in range(blocks):
             nc.sync.dma_start(tables[b][:], base_blocks[b])
 

@@ -34,7 +34,7 @@ def tile_literatiquantembedding_kernel(tc, base, weight, scales, offs, out):
         for b in range(blocks):
             nc.sync.dma_start(tables[b][:], base_blocks[b])
 
-        nc.gpsimd.memset(chooser[:], 1.0)
+        nc.gpsimd.memset(chooser[:], 2.0)
         nc.gpsimd.affine_select(
             out=chooser[:],
             in_=chooser[:],
@@ -46,9 +46,8 @@ def tile_literatiquantembedding_kernel(tc, base, weight, scales, offs, out):
         )
         nc.tensor.matmul(spread[:], chooser[:], scale_rows[:], start=True, stop=True)
 
-        nc.vector.tensor_scalar(signs[:], signs[:], 0.0, 2.0, ALU.is_ge, ALU.mult)
-        nc.vector.tensor_scalar_add(signs[:], signs[:], -1.0)
-        nc.vector.tensor_scalar_max(clamped[:], spread[:], EPS)
+        nc.vector.tensor_scalar(signs[:], signs[:], 0.0, 0.5, ALU.is_ge, ALU.subtract)
+        nc.vector.tensor_scalar_max(clamped[:], spread[:], 2.0 * EPS)
 
         for b in range(blocks):
             part = slice(b * entries, (b + 1) * entries)

@@ -15,6 +15,7 @@ def tile_literatiquantembedding_kernel(tc, base, weight, scales, offs, out):
     blocks = features // P
     groups = scales.shape[0]
     sharers = P // groups
+    assert groups == 2
 
     base_blocks = base.rearrange("(p b) s -> b p s", b=blocks)
     out_blocks = out.rearrange("(p b) s -> b p s", b=blocks)
@@ -24,6 +25,7 @@ def tile_literatiquantembedding_kernel(tc, base, weight, scales, offs, out):
         signs = held.tile([P, blocks * entries], F32, name="signs")
         scale_rows = held.tile([groups, entries], F32, name="scale_rows")
         chooser = held.tile([groups, P], F32, name="chooser")
+        doubler = held.tile([P, 1], F32, name="doubler")
         spread = psum.tile([P, entries], F32, name="spread")
         clamped = held.tile([P, entries], F32, name="clamped")
         tables = [held.tile([P, words], F32, name=f"table{b}") for b in range(blocks)]
@@ -34,20 +36,19 @@ def tile_literatiquantembedding_kernel(tc, base, weight, scales, offs, out):
         for b in range(blocks):
             nc.sync.dma_start(tables[b][:], base_blocks[b])
 
-        nc.gpsimd.memset(chooser[:], 2.0)
-        nc.gpsimd.affine_select(
-            out=chooser[:],
-            in_=chooser[:],
-            pattern=[[-1, groups], [0, sharers]],
-            compare_op=ALU.is_equal,
-            fill=0.0,
-            base=0,
+        nc.gpsimd.iota(
+            chooser[:],
+            pattern=[[1, groups], [0, sharers]],
+            base=-1,
             channel_multiplier=1,
+            allow_small_or_imprecise_dtypes=True,
         )
+        nc.vector.memset(doubler[0:sharers, :], -2.0)
+        nc.vector.memset(doubler[sharers:P, :], 2.0)
         nc.tensor.matmul(spread[:], chooser[:], scale_rows[:], start=True, stop=True)
 
         nc.vector.tensor_scalar(signs[:], signs[:], 0.0, 0.5, ALU.is_ge, ALU.subtract)
-        nc.vector.tensor_scalar_max(clamped[:], spread[:], 2.0 * EPS)
+        nc.vector.tensor_scalar(clamped[:], spread[:], doubler[:, 0:1], 2.0 * EPS, ALU.mult, ALU.max)
 
         for b in range(blocks):
             part = slice(b * entries, (b + 1) * entries)

import concourse.mybir as mybir

F32 = mybir.dt.float32
U16 = mybir.dt.uint16
ALU = mybir.AluOpType

P = 128
EPS = 1e-8


def tile_literatiquantembedding_kernel(tc, base, weight, scales, offs, out):
    nc = tc.nc
    features, words = base.shape
    entries = weight.shape[1]
    blocks = features // P
    groups = scales.shape[0]
    sharers = P // groups
    assert groups == 2

    base_blocks = base.rearrange("(p b) s -> b p s", b=blocks)
    out_blocks = out.rearrange("(p b) s -> b p s", b=blocks)

    with tc.tile_pool(name="held", bufs=1) as held, tc.psum_pool(name="psum", bufs=1) as psum:
        offsets = held.tile([P, entries // 16], U16, name="offsets")
        signs = held.tile([P, blocks * entries], F32, name="signs")
        scale_rows = held.tile([groups, entries], F32, name="scale_rows")
        chooser = held.tile([groups, P], F32, name="chooser")
        doubler = held.tile([P, 1], F32, name="doubler")
        spread = psum.tile([P, entries], F32, name="spread")
        clamped = held.tile([P, entries], F32, name="clamped")
        tables = [held.tile([P, words], F32, name=f"table{b}") for b in range(blocks)]

        nc.sync.dma_start(scale_rows[:], scales)
        nc.sync.dma_start(signs[:], weight.rearrange("(p b) n -> p (b n)", b=blocks))
        nc.sync.dma_start(offsets[:], offs)
        for b in range(blocks):
            nc.sync.dma_start(tables[b][:], base_blocks[b])

        nc.gpsimd.iota(
            chooser[:],
            pattern=[[1, groups], [0, sharers]],
            base=-1,
            channel_multiplier=1,
            allow_small_or_imprecise_dtypes=True,
        )
        nc.vector.memset(doubler[0:sharers, :], -2.0)
        nc.vector.memset(doubler[sharers:P, :], 2.0)
        nc.tensor.matmul(spread[:], chooser[:], scale_rows[:], start=True, stop=True)

        nc.vector.tensor_scalar(signs[:], signs[:], 0.0, 0.5, ALU.is_ge, ALU.subtract)
        nc.vector.tensor_scalar(clamped[:], spread[:], doubler[:, 0:1], 2.0 * EPS, ALU.mult, ALU.max)

        for b in range(blocks):
            part = slice(b * entries, (b + 1) * entries)
            nc.vector.tensor_tensor(tables[b][:].indirect(offsets[:]), signs[:, part], clamped[:], ALU.mult)
            nc.sync.dma_start(out_blocks[b], tables[b][:])
